import numpy as np
import ml_dtypes


def mxq(x, axis, fmt="e4m3"):
    dtype, down = {"e4m3": (ml_dtypes.float8_e4m3fn, 7), "e5m2": (ml_dtypes.float8_e5m2, 14)}[fmt]
    v = np.moveaxis(np.asarray(x, np.float32).astype(ml_dtypes.bfloat16).astype(np.float64), axis, -1)
    blocks = v.reshape(v.shape[:-1] + (-1, 32))
    amax = np.abs(blocks).max(-1, keepdims=True)
    byte = np.maximum(np.where(amax > 0, np.frexp(amax)[1] - 1 + 127, 0) - down, 1)
    scale = np.exp2(byte - 127.0)
    codes = (blocks / scale).astype(np.float32).astype(dtype).astype(np.float64)
    return np.moveaxis((codes * scale).reshape(v.shape), -1, axis)


WIDE = False


def mx_kscale(k):
    if not WIDE:
        return np.ones(k)
    levels = np.array([10, -10, 5, -5, 0])
    a = np.random.permutation(np.resize(levels, k // 512 * 4)).reshape(k // 512, 4)
    idx = np.arange(k)
    return np.exp2(a[idx // 512, idx % 128 // 32])


BF16 = ml_dtypes.bfloat16


def bf(x):
    return np.asarray(x, np.float32).astype(BF16)


def f64(x):
    return np.asarray(x).astype(np.float64)


N, M, D, DV = 2048, 2048, 512, 512
EPS = 1e-12


def setup_inputs():
    s = mx_kscale(D)
    return {"q": bf(np.random.standard_normal((N, D)) * 0.6 * s),
            "k": bf(np.random.standard_normal((M, D)) * 0.6 / s),
            "v": bf(np.random.standard_normal((M, DV)) * 0.6)}


def reference(q, k, v):
    s = mxq(f64(q), 1, "e4m3") @ mxq(f64(k), 1, "e4m3").T
    norm = np.sqrt(np.sum(s * s, axis=1, keepdims=True))
    w = s / np.maximum(norm, EPS)
    return mxq(w, 1, "e4m3") @ mxq(f64(v), 0, "e4m3")

@@ -1,0 +1,245 @@
+from contextlib import ExitStack
+
+import concourse.mybir as mybir
+from concourse.masks import make_identity
+
+F32 = mybir.dt.float32
+BF16 = mybir.dt.bfloat16
+U32 = mybir.dt.uint32
+U8 = mybir.dt.uint8
+FP8X4 = mybir.dt.float8_e4m3fn_x4
+ALU = mybir.AluOpType
+ACT = mybir.ActivationFunctionType
+
+P = 128
+PACK = 4
+CHUNK = P * PACK
+ROWS = 2048
+WIDTH = 512
+CHUNKS = ROWS // CHUNK
+BLOCKS = ROWS // P
+UNITS = BLOCKS * CHUNKS
+EPS = 1e-12
+FLOPS = 2 * ROWS * ROWS * WIDTH * 2
+
+SPREAD_LAG = 3
+WEIGHT_LAG = 7
+QUANT_LAG = WEIGHT_LAG + 1
+OUT_LAG = WEIGHT_LAG + 3
+
+
+def tile_selfattention_pa_kernel(tc, q, k, v, out):
+    nc = tc.nc
+    with ExitStack() as ctx:
+        keep = ctx.enter_context(tc.tile_pool(name="keep", bufs=1))
+        small = ctx.enter_context(tc.tile_pool(name="small", bufs=4))
+        scrap = ctx.enter_context(tc.tile_pool(name="scrap", bufs=4))
+        weights = ctx.enter_context(tc.tile_pool(name="weights", bufs=4))
+        stage = ctx.enter_context(tc.tile_pool(name="stage", bufs=4))
+        ps_norm = ctx.enter_context(tc.psum_pool(name="ps_norm", bufs=2))
+        ps_weight = ctx.enter_context(tc.psum_pool(name="ps_weight", bufs=3))
+        ps_out = ctx.enter_context(tc.psum_pool(name="ps_out", bufs=2))
+        ps_spread = ctx.enter_context(tc.psum_pool(name="ps_spread", bufs=1))
+
+        ctx.enter_context(tc.manual_schedule())
+
+        ident = keep.tile([P, P], F32, name="ident")
+        make_identity(nc, ident[:])
+        minus_half = keep.tile([P, 1], F32, name="minus_half")
+        nc.gpsimd.memset(minus_half[:], -0.5)
+
+        q_rows = q.rearrange("(g p t) d -> p g (t d)", p=P, t=PACK)
+        k_rows = k.rearrange("(g p t) d -> p g (t d)", p=P, t=PACK)
+        v_rows = v.rearrange("(g p t) d -> p g (t d)", p=P, t=PACK)
+        out_rows = out.rearrange("(g p t) d -> p g t d", p=P, t=PACK)
+
+        q_raw = keep.tile([P, ROWS * PACK], BF16, name="q_raw")
+        k_raw = keep.tile([P, ROWS * PACK], BF16, name="k_raw")
+        v_raw = keep.tile([P, ROWS * PACK], BF16, name="v_raw")
+        q_grouped = keep.tile([P, ROWS * PACK], BF16, name="q_grouped", align_bytes=64)
+        k_grouped = keep.tile([P, ROWS * PACK], BF16, name="k_grouped", align_bytes=64)
+        v_grouped = keep.tile([P, ROWS * PACK], BF16, name="v_grouped", align_bytes=64)
+        q_codes = keep.tile([P, ROWS], U32, name="q_codes", align_bytes=64)
+        k_codes = keep.tile([P, ROWS], U32, name="k_codes", align_bytes=64)
+        v_codes = keep.tile([P, ROWS], U32, name="v_codes", align_bytes=64)
+        q_scales = keep.tile([P, ROWS], U8, name="q_scales", align_bytes=64)
+        k_scales = keep.tile([P, ROWS], U8, name="k_scales", align_bytes=64)
+        v_scales = keep.tile([P, ROWS], U8, name="v_scales", align_bytes=64)
+
+        def load(raw, rows, g):
+            nc.sync.dma_start(out=raw[:, g * CHUNK * PACK : (g + 1) * CHUNK * PACK], in_=rows[:, g, :])
+
+        def transpose_chunk(raw, grouped, g):
+            raw_words = raw[:].bitcast(F32)
+            grouped_words = grouped[:].bitcast(F32).rearrange("p (r u) -> p r u", u=2)
+            for half in range(2):
+                bank = ps_weight.tile([P, 2, 2 * P], F32, tag="bank", name="flipped")
+                for t2 in range(2):
+                    first_word = (g * PACK + 2 * half + t2) * (WIDTH // 2)
+                    for u in range(2):
+                        nc.tensor.transpose(
+                            bank[:, u, t2 * P : (t2 + 1) * P],
+                            raw_words[:, first_word + u * P : first_word + (u + 1) * P],
+                            ident[:],
+                        )
+                first_col = g * CHUNK + half * 2 * P
+                dst = grouped_words[:, first_col : first_col + 2 * P, :]
+                src = bank[:].rearrange("p u r -> p r u")
+                if half == 0:
+                    nc.scalar.copy(out=dst, in_=src)
+                else:
+                    nc.vector.tensor_copy(out=dst, in_=src)
+
+        def quantise_chunk(grouped, codes, scales, g):
+            cols = slice(g * CHUNK, (g + 1) * CHUNK)
+            nc.vector.quantize_mx(
+                out=codes[:, cols].bitcast(FP8X4),
+                scales=scales[:, cols],
+                in_=grouped[:, g * CHUNK * PACK : (g + 1) * CHUNK * PACK],
+            )
+
+        def regroup_v(g):
+            part = slice(g * CHUNK * PACK, (g + 1) * CHUNK * PACK)
+            nc.vector.tensor_copy(
+                out=v_grouped[:, part].rearrange("p (c i t) -> p c t i", i=4, t=PACK),
+                in_=v_raw[:, part].rearrange("p (t c i) -> p c t i", i=4, t=PACK),
+            )
+
+        def query_cols(b):
+            return slice(b * P, (b + 1) * P)
+
+        squares = {}
+        inv_norm = {}
+        spread = {}
+        w_grouped = {}
+        w_codes = {}
+        w_scales = {}
+        acc = {}
+
+        def norm_pass(unit):
+            b, g = divmod(unit, CHUNKS)
+            if g == 0:
+                squares[b] = small.tile([P, CHUNKS], F32, name="squares")
+            key_cols = slice(g * CHUNK, (g + 1) * CHUNK)
+            bank = ps_norm.tile([P, CHUNK], F32, name="scores")
+            nc.tensor.matmul_mx(
+                out=bank[:],
+                lhsT=q_codes[:, query_cols(b)].bitcast(FP8X4),
+                lhsT_scale=q_scales[:, query_cols(b)],
+                rhs=k_codes[:, key_cols].bitcast(FP8X4),
+                rhs_scale=k_scales[:, key_cols],
+                start=True,
+                stop=True,
+            )
+            unread = scrap.tile([P, CHUNK], BF16, name="unread")
+            nc.scalar.activation(out=unread[:], in_=bank[:], func=ACT.Square, accum_out=squares[b][:, g : g + 1])
+
+        def norm_finish(b):
+            pair = small.tile([P, 2], F32, name="pair")
+            nc.gpsimd.tensor_tensor(out=pair[:], in0=squares[b][:, 0:2], in1=squares[b][:, 2:4], op=ALU.add)
+            total = small.tile([P, 1], F32, name="total")
+            nc.gpsimd.tensor_tensor(out=total[:], in0=pair[:, 0:1], in1=pair[:, 1:2], op=ALU.add)
+            floored = small.tile([P, 1], F32, name="floored")
+            nc.gpsimd.tensor_scalar_max(out=floored[:], in0=total[:], scalar1=EPS * EPS)
+            inv_norm[b] = small.tile([P, 1], F32, name="inv_norm")
+            nc.gpsimd.tensor_tensor(out=inv_norm[b][:], in0=floored[:], in1=minus_half[:], op=ALU.pow)
+
+        def spread_norm(b):
+            bank = ps_spread.tile([P, P], F32, name="spread_bank")
+            nc.tensor.matmul(
+                out=bank[:], lhsT=inv_norm[b][:, 0:1].to_broadcast([P, P]), rhs=ident[:], start=True, stop=True
+            )
+            spread[b] = small.tile([P, P], F32, name="spread")
+            nc.scalar.copy(out=spread[b][:], in_=bank[:])
+
+        def weight_pass(unit):
+            b, g = divmod(unit, CHUNKS)
+            if g == 0:
+                w_grouped[b] = weights.tile([P, CHUNKS, P, PACK], BF16, name="w_grouped", align_bytes=64)
+                w_codes[b] = weights.tile([P, CHUNK], U32, name="w_codes", align_bytes=64)
+                w_scales[b] = weights.tile([P, CHUNK], U8, name="w_scales", align_bytes=64)
+            bank = ps_weight.tile([P, PACK, P], F32, tag="bank", name="scores_t")
+            for t in range(PACK):
+                key_cols = slice(g * CHUNK + t * P, g * CHUNK + (t + 1) * P)
+                nc.tensor.matmul_mx(
+                    out=bank[:, t, :],
+                    lhsT=k_codes[:, key_cols].bitcast(FP8X4),
+                    lhsT_scale=k_scales[:, key_cols],
+                    rhs=q_codes[:, query_cols(b)].bitcast(FP8X4),
+                    rhs_scale=q_scales[:, query_cols(b)],
+                    start=True,
+                    stop=True,
+                )
+            nc.vector.tensor_tensor(
+                out=w_grouped[b][:, g, :, :],
+                in0=bank[:].rearrange("p t r -> p r t"),
+                in1=spread[b][:].unsqueeze(2).to_broadcast([P, P, PACK]),
+                op=ALU.mult,
+            )
+
+        def weight_quantise(unit):
+            b, g = divmod(unit, CHUNKS)
+            cols = slice(g * P, (g + 1) * P)
+            nc.vector.quantize_mx(
+                out=w_codes[b][:, cols].bitcast(FP8X4),
+                scales=w_scales[b][:, cols],
+                in_=w_grouped[b][:, g, :, :].rearrange("p r t -> p (r t)"),
+            )
+
+        def output_pass(unit):
+            b, g = divmod(unit, CHUNKS)
+            if g == 0:
+                acc[b] = ps_out.tile([P, WIDTH], F32, name="acc")
+            cols = slice(g * P, (g + 1) * P)
+            key_cols = slice(g * CHUNK, (g + 1) * CHUNK)
+            nc.tensor.matmul_mx(
+                out=acc[b][:],
+                lhsT=w_codes[b][:, cols].bitcast(FP8X4),
+                lhsT_scale=w_scales[b][:, cols],
+                rhs=v_codes[:, key_cols].bitcast(FP8X4),
+                rhs_scale=v_scales[:, key_cols],
+                start=(g == 0),
+                stop=(g == CHUNKS - 1),
+            )
+            if g == CHUNKS - 1:
+                result = stage.tile([P, WIDTH], F32, name="result")
+                nc.scalar.copy(out=result[:], in_=acc[b][:])
+                nc.sync.dma_start(out=out_rows[:, b // PACK, b % PACK, :], in_=result[:])
+
+        load(q_raw, q_rows, 0)
+        for g in range(CHUNKS):
+            load(k_raw, k_rows, g)
+        for g in range(CHUNKS):
+            load(v_raw, v_rows, g)
+        for g in range(1, CHUNKS):
+            load(q_raw, q_rows, g)
+
+        transpose_chunk(q_raw, q_grouped, 0)
+        transpose_chunk(k_raw, k_grouped, 0)
+        quantise_chunk(q_grouped, q_codes, q_scales, 0)
+        for g in range(1, CHUNKS):
+            transpose_chunk(k_raw, k_grouped, g)
+            quantise_chunk(k_grouped, k_codes, k_scales, g - 1)
+        quantise_chunk(k_grouped, k_codes, k_scales, CHUNKS - 1)
+
+        for step in range(UNITS + OUT_LAG):
+            if step < UNITS:
+                norm_pass(step)
+                if step % CHUNKS == CHUNKS - 1:
+                    norm_finish(step // CHUNKS)
+            if step < CHUNKS:
+                regroup_v(step)
+            if 1 <= step < CHUNKS + 1:
+                quantise_chunk(v_grouped, v_codes, v_scales, step - 1)
+            if step % (CHUNKS * PACK) == CHUNKS and step // (CHUNKS * PACK) + 1 < CHUNKS:
+                transpose_chunk(q_raw, q_grouped, step // (CHUNKS * PACK) + 1)
+            if step % (CHUNKS * PACK) == CHUNKS + 1 and step // (CHUNKS * PACK) + 1 < CHUNKS:
+                quantise_chunk(q_grouped, q_codes, q_scales, step // (CHUNKS * PACK) + 1)
+            if 0 <= step - SPREAD_LAG < UNITS and (step - SPREAD_LAG) % CHUNKS == CHUNKS - 1:
+                spread_norm((step - SPREAD_LAG) // CHUNKS)
+            if 0 <= step - WEIGHT_LAG < UNITS:
+                weight_pass(step - WEIGHT_LAG)
+            if 0 <= step - QUANT_LAG < UNITS:
+                weight_quantise(step - QUANT_LAG)
+            if 0 <= step - OUT_LAG < UNITS:
+                output_pass(step - OUT_LAG)

@@ -22,8 +22,8 @@ UNITS = BLOCKS * CHUNKS
 EPS = 1e-12
 FLOPS = 2 * ROWS * ROWS * WIDTH * 2
 
-SPREAD_LAG = 3
-WEIGHT_LAG = 7
+SPREAD_LAG = 7
+WEIGHT_LAG = 11
 QUANT_LAG = WEIGHT_LAG + 1
 OUT_LAG = WEIGHT_LAG + 3
 

@@ -146,9 +146,7 @@ def tile_selfattention_pa_kernel(tc, q, k, v, out):
 
         def spread_norm(b):
             bank = ps_spread.tile([P, P], F32, name="spread_bank")
-            nc.tensor.matmul(
-                out=bank[:], lhsT=inv_norm[b][:, 0:1].to_broadcast([P, P]), rhs=ident[:], start=True, stop=True
-            )
+            nc.tensor.transpose(bank[:], inv_norm[b][:, 0:1].to_broadcast([P, P]), ident[:])
             spread[b] = small.tile([P, P], F32, name="spread")
             nc.scalar.copy(out=spread[b][:], in_=bank[:])
 

@@ -22,24 +22,32 @@ UNITS = BLOCKS * CHUNKS
 EPS = 1e-12
 FLOPS = 2 * ROWS * ROWS * WIDTH * 2
 
-SPREAD_LAG = 7
-WEIGHT_LAG = 11
-QUANT_LAG = WEIGHT_LAG + 1
-OUT_LAG = WEIGHT_LAG + 3
+FIRST_NORMS = 15
+SPREAD_MAX = 2
+CHAIN_UNITS = 4
+SPREAD_AHEAD = 1
+OUT_LAG = 4
+STORE_LAG = 0
+NORM_SPAN = 52
+Q1_AT = 10
+Q1Q_AT = 3
+NB = 3
+WB = 3
+Q_STEP = 8
+Q_EVERY = 8
 
 
 def tile_selfattention_pa_kernel(tc, q, k, v, out):
     nc = tc.nc
     with ExitStack() as ctx:
         keep = ctx.enter_context(tc.tile_pool(name="keep", bufs=1))
-        small = ctx.enter_context(tc.tile_pool(name="small", bufs=4))
+        small = ctx.enter_context(tc.tile_pool(name="small", bufs=24))
         scrap = ctx.enter_context(tc.tile_pool(name="scrap", bufs=4))
         weights = ctx.enter_context(tc.tile_pool(name="weights", bufs=4))
         stage = ctx.enter_context(tc.tile_pool(name="stage", bufs=4))
-        ps_norm = ctx.enter_context(tc.psum_pool(name="ps_norm", bufs=2))
-        ps_weight = ctx.enter_context(tc.psum_pool(name="ps_weight", bufs=3))
+        ps_norm = ctx.enter_context(tc.psum_pool(name="ps_norm", bufs=NB))
+        ps_weight = ctx.enter_context(tc.psum_pool(name="ps_weight", bufs=WB))
         ps_out = ctx.enter_context(tc.psum_pool(name="ps_out", bufs=2))
-        ps_spread = ctx.enter_context(tc.psum_pool(name="ps_spread", bufs=1))
 
         ctx.enter_context(tc.manual_schedule())
 
@@ -48,12 +56,13 @@ def tile_selfattention_pa_kernel(tc, q, k, v, out):
         minus_half = keep.tile([P, 1], F32, name="minus_half")
         nc.gpsimd.memset(minus_half[:], -0.5)
 
-        q_rows = q.rearrange("(g p t) d -> p g (t d)", p=P, t=PACK)
         k_rows = k.rearrange("(g p t) d -> p g (t d)", p=P, t=PACK)
         v_rows = v.rearrange("(g p t) d -> p g (t d)", p=P, t=PACK)
-        out_rows = out.rearrange("(g p t) d -> p g t d", p=P, t=PACK)
+        q_rows = q.rearrange("(b p) d -> p b d", p=P)
+        out_rows = out.rearrange("(b p) d -> p b d", p=P)
+        q_seg = q.rearrange("r (u s i) -> (r u) s i", u=2, s=4).rearrange("(m j) s i -> s j m i", j=32)
 
-        q_raw = keep.tile([P, ROWS * PACK], BF16, name="q_raw")
+        q_raw = keep.tile([P, ROWS * PACK], BF16, name="q_raw", align_bytes=64)
         k_raw = keep.tile([P, ROWS * PACK], BF16, name="k_raw")
         v_raw = keep.tile([P, ROWS * PACK], BF16, name="v_raw")
         q_grouped = keep.tile([P, ROWS * PACK], BF16, name="q_grouped", align_bytes=64)
@@ -69,34 +78,43 @@ def tile_selfattention_pa_kernel(tc, q, k, v, out):
         def load(raw, rows, g):
             nc.sync.dma_start(out=raw[:, g * CHUNK * PACK : (g + 1) * CHUNK * PACK], in_=rows[:, g, :])
 
-        def transpose_chunk(raw, grouped, g):
+        flips = [0]
+
+        def flip_bank():
+            flips[0] += 1
+            if flips[0] <= 9 and flips[0] % 5 >= 3:
+                return ps_out.tile([P, 2, 2 * P], F32, tag="acc", name="flipped_early")
+            return ps_weight.tile([P, 2, 2 * P], F32, tag="bank", name="flipped")
+
+        def transpose_half(raw, grouped, g, half, copy):
             raw_words = raw[:].bitcast(F32)
             grouped_words = grouped[:].bitcast(F32).rearrange("p (r u) -> p r u", u=2)
-            for half in range(2):
-                bank = ps_weight.tile([P, 2, 2 * P], F32, tag="bank", name="flipped")
-                for t2 in range(2):
-                    first_word = (g * PACK + 2 * half + t2) * (WIDTH // 2)
-                    for u in range(2):
-                        nc.tensor.transpose(
-                            bank[:, u, t2 * P : (t2 + 1) * P],
-                            raw_words[:, first_word + u * P : first_word + (u + 1) * P],
-                            ident[:],
-                        )
-                first_col = g * CHUNK + half * 2 * P
-                dst = grouped_words[:, first_col : first_col + 2 * P, :]
-                src = bank[:].rearrange("p u r -> p r u")
-                if half == 0:
-                    nc.scalar.copy(out=dst, in_=src)
-                else:
-                    nc.vector.tensor_copy(out=dst, in_=src)
+            bank = flip_bank()
+            for t2 in range(2):
+                first_word = (g * PACK + 2 * half + t2) * (WIDTH // 2)
+                for u in range(2):
+                    nc.tensor.transpose(
+                        bank[:, u, t2 * P : (t2 + 1) * P],
+                        raw_words[:, first_word + u * P : first_word + (u + 1) * P],
+                        ident[:],
+                    )
+            first_col = g * CHUNK + half * 2 * P
+            copy(
+                out=grouped_words[:, first_col : first_col + 2 * P, :],
+                in_=bank[:].rearrange("p u r -> p r u"),
+            )
+
+        def transpose_chunk(raw, grouped, g):
+            transpose_half(raw, grouped, g, 0, nc.scalar.copy)
+            transpose_half(raw, grouped, g, 1, nc.vector.tensor_copy)
+
+        def quantise_cols(grouped, codes, scales, lo, hi):
+            nc.vector.quantize_mx(
+                out=codes[:, lo:hi].bitcast(FP8X4), scales=scales[:, lo:hi], in_=grouped[:, lo * PACK : hi * PACK]
+            )
 
         def quantise_chunk(grouped, codes, scales, g):
-            cols = slice(g * CHUNK, (g + 1) * CHUNK)
-            nc.vector.quantize_mx(
-                out=codes[:, cols].bitcast(FP8X4),
-                scales=scales[:, cols],
-                in_=grouped[:, g * CHUNK * PACK : (g + 1) * CHUNK * PACK],
-            )
+            quantise_cols(grouped, codes, scales, g * CHUNK, (g + 1) * CHUNK)
 
         def regroup_v(g):
             part = slice(g * CHUNK * PACK, (g + 1) * CHUNK * PACK)
@@ -104,6 +122,10 @@ def tile_selfattention_pa_kernel(tc, q, k, v, out):
                 out=v_grouped[:, part].rearrange("p (c i t) -> p c t i", i=4, t=PACK),
                 in_=v_raw[:, part].rearrange("p (t c i) -> p c t i", i=4, t=PACK),
             )
+
+        def turn_q(g):
+            cols = slice(g * CHUNK * PACK, (g + 1) * CHUNK * PACK)
+            nc.vector.transpose(q_grouped[:, cols].bitcast(F32), q_raw[:, cols].bitcast(F32))
 
         def query_cols(b):
             return slice(b * P, (b + 1) * P)
@@ -116,12 +138,11 @@ def tile_selfattention_pa_kernel(tc, q, k, v, out):
         w_scales = {}
         acc = {}
 
-        def norm_pass(unit):
-            b, g = divmod(unit, CHUNKS)
-            if g == 0:
+        def norm_pass(b, g):
+            if b not in squares:
                 squares[b] = small.tile([P, CHUNKS], F32, name="squares")
             key_cols = slice(g * CHUNK, (g + 1) * CHUNK)
-            bank = ps_norm.tile([P, CHUNK], F32, name="scores")
+            bank = ps_norm.tile([P, CHUNK], F32, tag="scores", name="scores")
             nc.tensor.matmul_mx(
                 out=bank[:],
                 lhsT=q_codes[:, query_cols(b)].bitcast(FP8X4),
@@ -137,18 +158,20 @@ def tile_selfattention_pa_kernel(tc, q, k, v, out):
         def norm_finish(b):
             pair = small.tile([P, 2], F32, name="pair")
             nc.gpsimd.tensor_tensor(out=pair[:], in0=squares[b][:, 0:2], in1=squares[b][:, 2:4], op=ALU.add)
-            total = small.tile([P, 1], F32, name="total")
-            nc.gpsimd.tensor_tensor(out=total[:], in0=pair[:, 0:1], in1=pair[:, 1:2], op=ALU.add)
             floored = small.tile([P, 1], F32, name="floored")
-            nc.gpsimd.tensor_scalar_max(out=floored[:], in0=total[:], scalar1=EPS * EPS)
+            nc.gpsimd.tensor_scalar(
+                out=floored[:], in0=pair[:, 0:1], scalar1=pair[:, 1:2], scalar2=EPS * EPS, op0=ALU.add, op1=ALU.max
+            )
             inv_norm[b] = small.tile([P, 1], F32, name="inv_norm")
             nc.gpsimd.tensor_tensor(out=inv_norm[b][:], in0=floored[:], in1=minus_half[:], op=ALU.pow)
 
-        def spread_norm(b):
-            bank = ps_spread.tile([P, P], F32, name="spread_bank")
-            nc.tensor.transpose(bank[:], inv_norm[b][:, 0:1].to_broadcast([P, P]), ident[:])
-            spread[b] = small.tile([P, P], F32, name="spread")
-            nc.scalar.copy(out=spread[b][:], in_=bank[:])
+        def spread_norms(blocks):
+            bank = ps_weight.tile([P, SPREAD_MAX, P], F32, tag="bank", name="spread_bank")
+            tile = small.tile([P, SPREAD_MAX, P], F32, name="spread")
+            for i, b in enumerate(blocks):
+                nc.tensor.transpose(bank[:, i, :], inv_norm[b][:, 0:1].to_broadcast([P, P]), ident[:])
+                spread[b] = tile[:, i, :]
+            nc.scalar.copy(out=tile[:, 0 : len(blocks), :], in_=bank[:, 0 : len(blocks), :])
 
         def weight_pass(unit):
             b, g = divmod(unit, CHUNKS)
@@ -171,7 +194,7 @@ def tile_selfattention_pa_kernel(tc, q, k, v, out):
             nc.vector.tensor_tensor(
                 out=w_grouped[b][:, g, :, :],
                 in0=bank[:].rearrange("p t r -> p r t"),
-                in1=spread[b][:].unsqueeze(2).to_broadcast([P, P, PACK]),
+                in1=spread[b].unsqueeze(2).to_broadcast([P, P, PACK]),
                 op=ALU.mult,
             )
 
@@ -187,7 +210,7 @@ def tile_selfattention_pa_kernel(tc, q, k, v, out):
         def output_pass(unit):
             b, g = divmod(unit, CHUNKS)
             if g == 0:
-                acc[b] = ps_out.tile([P, WIDTH], F32, name="acc")
+                acc[b] = ps_out.tile([P, WIDTH], F32, tag="acc", name="acc")
             cols = slice(g * P, (g + 1) * P)
             key_cols = slice(g * CHUNK, (g + 1) * CHUNK)
             nc.tensor.matmul_mx(
@@ -199,45 +222,95 @@ def tile_selfattention_pa_kernel(tc, q, k, v, out):
                 start=(g == 0),
                 stop=(g == CHUNKS - 1),
             )
-            if g == CHUNKS - 1:
-                result = stage.tile([P, WIDTH], F32, name="result")
-                nc.scalar.copy(out=result[:], in_=acc[b][:])
-                nc.sync.dma_start(out=out_rows[:, b // PACK, b % PACK, :], in_=result[:])
 
-        load(q_raw, q_rows, 0)
+        def store(b):
+            result = stage.tile([P, WIDTH], F32, name="result")
+            nc.scalar.copy(out=result[:], in_=acc[b][:])
+            nc.sync.dma_start(out=out_rows[:, b, :], in_=result[:])
+
+        norm_order = [(b, g) for b in range(BLOCKS) for g in range(CHUNKS)]
+        norms_done = []
+
+        def run_norms(count):
+            while len(norms_done) < min(count, UNITS):
+                b, g = norm_order[len(norms_done)]
+                norm_pass(b, g)
+                norms_done.append((b, g))
+                if g == CHUNKS - 1:
+                    norm_finish(b)
+
+        def load_q(b0, b1):
+            nc.sync.dma_start(out=q_raw[:, b0 * WIDTH : b1 * WIDTH].rearrange("p (b d) -> p b d", d=WIDTH), in_=q_rows[:, b0:b1, :])
+
+        load_q(0, 2)
         for g in range(CHUNKS):
             load(k_raw, k_rows, g)
+        load_q(2, 4)
         for g in range(CHUNKS):
             load(v_raw, v_rows, g)
-        for g in range(1, CHUNKS):
-            load(q_raw, q_rows, g)
+        load_q(4, 8)
+        for s in range(4):
+            nc.sync.dma_start(
+                out=q_raw[32 * s : 32 * s + 32, 2 * CHUNK * PACK :].rearrange("p (m i) -> p m i", i=64),
+                in_=q_seg[s, :, 64:, :],
+            )
 
-        transpose_chunk(q_raw, q_grouped, 0)
-        transpose_chunk(k_raw, k_grouped, 0)
-        quantise_chunk(q_grouped, q_codes, q_scales, 0)
-        for g in range(1, CHUNKS):
+        transpose_half(q_raw, q_grouped, 0, 0, nc.scalar.copy)
+        quantise_cols(q_grouped, q_codes, q_scales, 0, 2 * P)
+        for g in range(CHUNKS):
             transpose_chunk(k_raw, k_grouped, g)
-            quantise_chunk(k_grouped, k_codes, k_scales, g - 1)
+            if g >= 1:
+                quantise_chunk(k_grouped, k_codes, k_scales, g - 1)
+            run_norms(g - 2)
         quantise_chunk(k_grouped, k_codes, k_scales, CHUNKS - 1)
+        for n in range(2, CHUNKS + 1):
+            run_norms(n)
+            if n == 3:
+                transpose_half(q_raw, q_grouped, 0, 1, nc.scalar.copy)
+        quantise_cols(q_grouped, q_codes, q_scales, 2 * P, 4 * P)
+        for n in range(CHUNKS + 1, FIRST_NORMS):
+            run_norms(n + 1)
+            if n == Q1_AT:
+                transpose_half(q_raw, q_grouped, 1, 0, nc.scalar.copy)
+                transpose_half(q_raw, q_grouped, 1, 1, nc.scalar.copy)
+        for g in range(CHUNKS):
+            regroup_v(g)
+            if g > 0:
+                quantise_chunk(v_grouped, v_codes, v_scales, g - 1)
+            if g == Q1Q_AT:
+                quantise_chunk(q_grouped, q_codes, q_scales, 1)
+        quantise_chunk(v_grouped, v_codes, v_scales, CHUNKS - 1)
 
-        for step in range(UNITS + OUT_LAG):
+        size = min(SPREAD_MAX, max(1, (FIRST_NORMS - CHAIN_UNITS) // CHUNKS))
+        spread_norms(range(size))
+        next_spread = size
+        outs_done = 0
+        stores_done = 0
+        store_after = {}
+
+        step = 0
+        while stores_done < BLOCKS:
             if step < UNITS:
-                norm_pass(step)
-                if step % CHUNKS == CHUNKS - 1:
-                    norm_finish(step // CHUNKS)
-            if step < CHUNKS:
-                regroup_v(step)
-            if 1 <= step < CHUNKS + 1:
-                quantise_chunk(v_grouped, v_codes, v_scales, step - 1)
-            if step % (CHUNKS * PACK) == CHUNKS and step // (CHUNKS * PACK) + 1 < CHUNKS:
-                transpose_chunk(q_raw, q_grouped, step // (CHUNKS * PACK) + 1)
-            if step % (CHUNKS * PACK) == CHUNKS + 1 and step // (CHUNKS * PACK) + 1 < CHUNKS:
-                quantise_chunk(q_grouped, q_codes, q_scales, step // (CHUNKS * PACK) + 1)
-            if 0 <= step - SPREAD_LAG < UNITS and (step - SPREAD_LAG) % CHUNKS == CHUNKS - 1:
-                spread_norm((step - SPREAD_LAG) // CHUNKS)
-            if 0 <= step - WEIGHT_LAG < UNITS:
-                weight_pass(step - WEIGHT_LAG)
-            if 0 <= step - QUANT_LAG < UNITS:
-                weight_quantise(step - QUANT_LAG)
-            if 0 <= step - OUT_LAG < UNITS:
-                output_pass(step - OUT_LAG)
+                weight_pass(step)
+            if 1 <= step < UNITS + 1:
+                weight_quantise(step - 1)
+            run_norms(FIRST_NORMS + (UNITS - FIRST_NORMS) * (step + 1) // NORM_SPAN)
+            for g in (2, 3):
+                if step == Q_STEP + (g - 2) * Q_EVERY:
+                    turn_q(g)
+                if step == Q_STEP + (g - 2) * Q_EVERY + 2:
+                    quantise_chunk(q_grouped, q_codes, q_scales, g)
+            if next_spread < BLOCKS and step + SPREAD_AHEAD >= next_spread * CHUNKS:
+                ready = max((len(norms_done) - CHAIN_UNITS) // CHUNKS, next_spread + 1)
+                size = min(ready - next_spread, SPREAD_MAX)
+                spread_norms(range(next_spread, next_spread + size))
+                next_spread += size
+            if outs_done < UNITS and outs_done <= step - OUT_LAG:
+                output_pass(outs_done)
+                if outs_done % CHUNKS == CHUNKS - 1:
+                    store_after[outs_done // CHUNKS] = step + STORE_LAG
+                outs_done += 1
+            if stores_done in store_after and step >= store_after[stores_done]:
+                store(stores_done)
+                stores_done += 1
+            step += 1

@@ -33,8 +33,8 @@ Q1_AT = 10
 Q1Q_AT = 3
 NB = 3
 WB = 3
-Q_STEP = 8
-Q_EVERY = 8
+Q_STEP = 14
+Q_EVERY = 14
 
 
 def tile_selfattention_pa_kernel(tc, q, k, v, out):
@@ -44,7 +44,7 @@ def tile_selfattention_pa_kernel(tc, q, k, v, out):
         small = ctx.enter_context(tc.tile_pool(name="small", bufs=24))
         scrap = ctx.enter_context(tc.tile_pool(name="scrap", bufs=4))
         weights = ctx.enter_context(tc.tile_pool(name="weights", bufs=4))
-        stage = ctx.enter_context(tc.tile_pool(name="stage", bufs=4))
+        stage = ctx.enter_context(tc.tile_pool(name="stage", bufs=8))
         ps_norm = ctx.enter_context(tc.psum_pool(name="ps_norm", bufs=NB))
         ps_weight = ctx.enter_context(tc.psum_pool(name="ps_weight", bufs=WB))
         ps_out = ctx.enter_context(tc.psum_pool(name="ps_out", bufs=2))
@@ -249,11 +249,12 @@ def tile_selfattention_pa_kernel(tc, q, k, v, out):
         for g in range(CHUNKS):
             load(v_raw, v_rows, g)
         load_q(4, 8)
-        for s in range(4):
-            nc.sync.dma_start(
-                out=q_raw[32 * s : 32 * s + 32, 2 * CHUNK * PACK :].rearrange("p (m i) -> p m i", i=64),
-                in_=q_seg[s, :, 64:, :],
-            )
+        for g in (2, 3):
+            for s in range(4):
+                nc.sync.dma_start(
+                    out=q_raw[32 * s : 32 * s + 32, g * CHUNK * PACK : (g + 1) * CHUNK * PACK].rearrange("p (m i) -> p m i", i=64),
+                    in_=q_seg[s, :, 32 * g : 32 * g + 32, :],
+                )
 
         transpose_half(q_raw, q_grouped, 0, 0, nc.scalar.copy)
         quantise_cols(q_grouped, q_codes, q_scales, 0, 2 * P)

@@ -22,19 +22,21 @@ UNITS = BLOCKS * CHUNKS
 EPS = 1e-12
 FLOPS = 2 * ROWS * ROWS * WIDTH * 2
 
-FIRST_NORMS = 15
-SPREAD_MAX = 2
-CHAIN_UNITS = 4
-SPREAD_AHEAD = 1
+FIRST_NORMS = 13
+SPREAD_MAX = 3
+CHAIN_UNITS = 3
+SPREAD_AHEAD = 2
 OUT_LAG = 4
-STORE_LAG = 0
-NORM_SPAN = 52
+STORE_LAG = 1
+NORM_SPAN = 50
 Q1_AT = 10
+S_BOTH = (0,)
 Q1Q_AT = 3
 NB = 3
 WB = 3
 Q_STEP = 14
 Q_EVERY = 14
+WARM_UP = 5
 
 
 def tile_selfattention_pa_kernel(tc, q, k, v, out):
@@ -74,6 +76,12 @@ def tile_selfattention_pa_kernel(tc, q, k, v, out):
         q_scales = keep.tile([P, ROWS], U8, name="q_scales", align_bytes=64)
         k_scales = keep.tile([P, ROWS], U8, name="k_scales", align_bytes=64)
         v_scales = keep.tile([P, ROWS], U8, name="v_scales", align_bytes=64)
+
+        idle = keep.tile([P, WIDTH], BF16, name="idle")
+        nc.vector.memset(idle[:], 0.0)
+        for i in range(WARM_UP):
+            bank = ps_norm.tile([P, WIDTH], F32, tag="scores", name="unused")
+            nc.tensor.matmul(bank[:], lhsT=idle[:, 0:P], rhs=idle[:], start=True, stop=True)
 
         def load(raw, rows, g):
             nc.sync.dma_start(out=raw[:, g * CHUNK * PACK : (g + 1) * CHUNK * PACK], in_=rows[:, g, :])
@@ -259,25 +267,23 @@ def tile_selfattention_pa_kernel(tc, q, k, v, out):
         transpose_half(q_raw, q_grouped, 0, 0, nc.scalar.copy)
         quantise_cols(q_grouped, q_codes, q_scales, 0, 2 * P)
         for g in range(CHUNKS):
-            transpose_chunk(k_raw, k_grouped, g)
+            transpose_half(k_raw, k_grouped, g, 0, nc.scalar.copy)
+            transpose_half(k_raw, k_grouped, g, 1, nc.scalar.copy if g in S_BOTH else nc.vector.tensor_copy)
             if g >= 1:
                 quantise_chunk(k_grouped, k_codes, k_scales, g - 1)
-            run_norms(g - 2)
+        run_norms(2)
         quantise_chunk(k_grouped, k_codes, k_scales, CHUNKS - 1)
-        for n in range(2, CHUNKS + 1):
-            run_norms(n)
-            if n == 3:
-                transpose_half(q_raw, q_grouped, 0, 1, nc.scalar.copy)
+        regroup_v(0)
+        run_norms(3)
+        transpose_half(q_raw, q_grouped, 0, 1, nc.scalar.copy)
         quantise_cols(q_grouped, q_codes, q_scales, 2 * P, 4 * P)
-        for n in range(CHUNKS + 1, FIRST_NORMS):
-            run_norms(n + 1)
-            if n == Q1_AT:
-                transpose_half(q_raw, q_grouped, 1, 0, nc.scalar.copy)
-                transpose_half(q_raw, q_grouped, 1, 1, nc.scalar.copy)
-        for g in range(CHUNKS):
+        run_norms(Q1_AT + 1)
+        transpose_half(q_raw, q_grouped, 1, 0, nc.scalar.copy)
+        transpose_half(q_raw, q_grouped, 1, 1, nc.scalar.copy)
+        run_norms(FIRST_NORMS)
+        for g in range(1, CHUNKS):
             regroup_v(g)
-            if g > 0:
-                quantise_chunk(v_grouped, v_codes, v_scales, g - 1)
+            quantise_chunk(v_grouped, v_codes, v_scales, g - 1)
             if g == Q1Q_AT:
                 quantise_chunk(q_grouped, q_codes, q_scales, 1)
         quantise_chunk(v_grouped, v_codes, v_scales, CHUNKS - 1)

@@ -79,9 +79,13 @@ def tile_selfattention_pa_kernel(tc, q, k, v, out):
 
         idle = keep.tile([P, WIDTH], BF16, name="idle")
         nc.vector.memset(idle[:], 0.0)
-        for i in range(WARM_UP):
-            bank = ps_norm.tile([P, WIDTH], F32, tag="scores", name="unused")
-            nc.tensor.matmul(bank[:], lhsT=idle[:, 0:P], rhs=idle[:], start=True, stop=True)
+
+        def keep_warm(count):
+            for i in range(count):
+                bank = ps_norm.tile([P, WIDTH], F32, tag="scores", name="unused")
+                nc.tensor.matmul(bank[:], lhsT=idle[:, 0:P], rhs=idle[:], start=True, stop=True)
+
+        keep_warm(WARM_UP)
 
         def load(raw, rows, g):
             nc.sync.dma_start(out=raw[:, g * CHUNK * PACK : (g + 1) * CHUNK * PACK], in_=rows[:, g, :])
@@ -267,6 +271,7 @@ def tile_selfattention_pa_kernel(tc, q, k, v, out):
         transpose_half(q_raw, q_grouped, 0, 0, nc.scalar.copy)
         quantise_cols(q_grouped, q_codes, q_scales, 0, 2 * P)
         for g in range(CHUNKS):
+            keep_warm(1)
             transpose_half(k_raw, k_grouped, g, 0, nc.scalar.copy)
             transpose_half(k_raw, k_grouped, g, 1, nc.scalar.copy if g in S_BOTH else nc.vector.tensor_copy)
             if g >= 1:

@@ -23,19 +23,38 @@ EPS = 1e-12
 FLOPS = 2 * ROWS * ROWS * WIDTH * 2
 
 FIRST_NORMS = 13
-SPREAD_MAX = 3
-CHAIN_UNITS = 3
-SPREAD_AHEAD = 2
+SPREAD_MAX = 2
+CHAIN_UNITS = 2
+SPREAD_AHEAD = 1
 OUT_LAG = 4
 STORE_LAG = 1
-NORM_SPAN = 50
-Q1_AT = 10
-S_BOTH = (0,)
+NORM_SPAN = 48
+Q1_AT = 9
+S_BOTH = (0, 1)
 Q1Q_AT = 3
 NB = 3
 WB = 3
-Q_STEP = 14
-Q_EVERY = 14
+Q_STEP = 13
+Q_EVERY = 10
+ROW_BLOCKS = (15,)
+Q_UNITS = 1
+LAST_UNITS = 1
+Q2_DVE = 1
+Q3_DVE = 1
+S_REG = ()
+V_BOTH = ()
+Q_EV = 1
+Q1_EV = 0
+Q23_AT = 2
+KW = 0
+N_FIRST = 1
+REG0 = 0
+ROW_START = 50
+ROW_Q = 6
+O_BEFORE = 1
+N_BEFORE = 1
+Q01_EV = 1
+OUT_RATE = 1
 WARM_UP = 5
 
 
@@ -130,7 +149,7 @@ def tile_selfattention_pa_kernel(tc, q, k, v, out):
 
         def regroup_v(g):
             part = slice(g * CHUNK * PACK, (g + 1) * CHUNK * PACK)
-            nc.vector.tensor_copy(
+            (nc.scalar.copy if g in S_REG else nc.vector.tensor_copy)(
                 out=v_grouped[:, part].rearrange("p (c i t) -> p c t i", i=4, t=PACK),
                 in_=v_raw[:, part].rearrange("p (t c i) -> p c t i", i=4, t=PACK),
             )
@@ -185,8 +204,51 @@ def tile_selfattention_pa_kernel(tc, q, k, v, out):
                 spread[b] = tile[:, i, :]
             nc.scalar.copy(out=tile[:, 0 : len(blocks), :], in_=bank[:, 0 : len(blocks), :])
 
+        w_rows = {}
+
+        def row_pass(b, g):
+            if g == 0:
+                w_rows[b] = weights.tile([P, CHUNKS, 2, P, 2], BF16, name="w_rows", align_bytes=64)
+                w_grouped[b] = weights.tile([P, CHUNKS, P, PACK], BF16, name="w_grouped", align_bytes=64)
+                w_codes[b] = weights.tile([P, CHUNK], U32, name="w_codes", align_bytes=64)
+                w_scales[b] = weights.tile([P, CHUNK], U8, name="w_scales", align_bytes=64)
+            key_cols = slice(g * CHUNK, (g + 1) * CHUNK)
+            bank = ps_norm.tile([P, CHUNK], F32, tag="scores", name="scores")
+            nc.tensor.matmul_mx(
+                out=bank[:],
+                lhsT=q_codes[:, query_cols(b)].bitcast(FP8X4),
+                lhsT_scale=q_scales[:, query_cols(b)],
+                rhs=k_codes[:, key_cols].bitcast(FP8X4),
+                rhs_scale=k_scales[:, key_cols],
+                start=True,
+                stop=True,
+            )
+            for u in range(2):
+                half = bank[:, u * 2 * P : (u + 1) * 2 * P].rearrange("q (e p) -> q p e", e=2)
+                nc.scalar.activation(out=w_rows[b][:, g, u, :, :], in_=half, func=ACT.Copy, scale=inv_norm[b][:])
+
+        def row_turn(b, g):
+            words = w_rows[b][:].rearrange("q g u p e -> q (g u p e)").bitcast(F32)
+            bank = ps_norm.tile([P, 2, 2, P], F32, tag="scores", name="turned")
+            for i in range(2):
+                for u in range(2):
+                    first = ((g + i) * 2 + u) * P
+                    nc.tensor.transpose(bank[:, i, u, :], words[:, first : first + P], ident[:])
+            grouped_words = w_grouped[b][:].rearrange("p g r t -> p (g r t)").bitcast(F32)
+            nc.scalar.copy(
+                out=grouped_words[:, g * 2 * P : (g + 2) * 2 * P].rearrange("p (g r u) -> p g r u", g=2, u=2),
+                in_=bank[:].rearrange("p g u r -> p g r u"),
+            )
+
+        def row_quantise(b):
+            nc.vector.quantize_mx(
+                out=w_codes[b][:].bitcast(FP8X4),
+                scales=w_scales[b][:],
+                in_=w_grouped[b][:].rearrange("p g r t -> p (g r t)"),
+            )
+
         def weight_pass(unit):
-            b, g = divmod(unit, CHUNKS)
+            b, g = columns[unit // CHUNKS], unit % CHUNKS
             if g == 0:
                 w_grouped[b] = weights.tile([P, CHUNKS, P, PACK], BF16, name="w_grouped", align_bytes=64)
                 w_codes[b] = weights.tile([P, CHUNK], U32, name="w_codes", align_bytes=64)
@@ -211,16 +273,17 @@ def tile_selfattention_pa_kernel(tc, q, k, v, out):
             )
 
         def weight_quantise(unit):
-            b, g = divmod(unit, CHUNKS)
-            cols = slice(g * P, (g + 1) * P)
-            nc.vector.quantize_mx(
-                out=w_codes[b][:, cols].bitcast(FP8X4),
-                scales=w_scales[b][:, cols],
-                in_=w_grouped[b][:, g, :, :].rearrange("p r t -> p (r t)"),
-            )
+            b, g = columns[unit // CHUNKS], unit % CHUNKS
+            size = LAST_UNITS if b == columns[-1] else Q_UNITS
+            if (g + 1) % size == 0:
+                lo, hi = g + 1 - size, g + 1
+                nc.vector.quantize_mx(
+                    out=w_codes[b][:, lo * P : hi * P].bitcast(FP8X4),
+                    scales=w_scales[b][:, lo * P : hi * P],
+                    in_=w_grouped[b][:, lo:hi, :, :].rearrange("p g r t -> p (g r t)"),
+                )
 
-        def output_pass(unit):
-            b, g = divmod(unit, CHUNKS)
+        def output_pass(b, g):
             if g == 0:
                 acc[b] = ps_out.tile([P, WIDTH], F32, tag="acc", name="acc")
             cols = slice(g * P, (g + 1) * P)
@@ -240,7 +303,17 @@ def tile_selfattention_pa_kernel(tc, q, k, v, out):
             nc.scalar.copy(out=result[:], in_=acc[b][:])
             nc.sync.dma_start(out=out_rows[:, b, :], in_=result[:])
 
-        norm_order = [(b, g) for b in range(BLOCKS) for g in range(CHUNKS)]
+        columns = [b for b in range(BLOCKS) if b not in ROW_BLOCKS]
+        cut_n, cut_o = len(columns) - N_BEFORE, len(columns) - O_BEFORE
+        norm_blocks = columns[:cut_n] + list(ROW_BLOCKS) + columns[cut_n:]
+        out_blocks = columns[:cut_o] + list(ROW_BLOCKS) + columns[cut_o:]
+        w_units = len(columns) * CHUNKS
+        norm_order = [(b, g) for b in norm_blocks for g in range(CHUNKS)]
+        out_order = [(b, g) for b in out_blocks for g in range(CHUNKS)]
+
+        def norm_ready(b):
+            return len(norms_done) >= CHUNKS * (norm_blocks.index(b) + 1) + CHAIN_UNITS
+
         norms_done = []
 
         def run_norms(count):
@@ -262,29 +335,36 @@ def tile_selfattention_pa_kernel(tc, q, k, v, out):
             load(v_raw, v_rows, g)
         load_q(4, 8)
         for g in (2, 3):
+            if not (Q2_DVE, Q3_DVE)[g - 2]:
+                load_q(4 * g, 4 * g + 4)
+                continue
             for s in range(4):
                 nc.sync.dma_start(
                     out=q_raw[32 * s : 32 * s + 32, g * CHUNK * PACK : (g + 1) * CHUNK * PACK].rearrange("p (m i) -> p m i", i=64),
                     in_=q_seg[s, :, 32 * g : 32 * g + 32, :],
                 )
 
-        transpose_half(q_raw, q_grouped, 0, 0, nc.scalar.copy)
+        ev = (nc.scalar.copy, nc.vector.tensor_copy)
+        transpose_half(q_raw, q_grouped, 0, 0, ev[Q01_EV])
         quantise_cols(q_grouped, q_codes, q_scales, 0, 2 * P)
         for g in range(CHUNKS):
-            keep_warm(1)
-            transpose_half(k_raw, k_grouped, g, 0, nc.scalar.copy)
-            transpose_half(k_raw, k_grouped, g, 1, nc.scalar.copy if g in S_BOTH else nc.vector.tensor_copy)
+            keep_warm(KW)
+            transpose_half(k_raw, k_grouped, g, 0, ev[1] if g in V_BOTH else ev[0])
+            transpose_half(k_raw, k_grouped, g, 1, ev[0] if g in S_BOTH else ev[1])
             if g >= 1:
                 quantise_chunk(k_grouped, k_codes, k_scales, g - 1)
-        run_norms(2)
+        run_norms(N_FIRST)
         quantise_chunk(k_grouped, k_codes, k_scales, CHUNKS - 1)
-        regroup_v(0)
-        run_norms(3)
-        transpose_half(q_raw, q_grouped, 0, 1, nc.scalar.copy)
+        if REG0 == 0:
+            regroup_v(0)
+        run_norms(Q23_AT)
+        transpose_half(q_raw, q_grouped, 0, 1, ev[0])
         quantise_cols(q_grouped, q_codes, q_scales, 2 * P, 4 * P)
+        if REG0 == 1:
+            regroup_v(0)
         run_norms(Q1_AT + 1)
-        transpose_half(q_raw, q_grouped, 1, 0, nc.scalar.copy)
-        transpose_half(q_raw, q_grouped, 1, 1, nc.scalar.copy)
+        transpose_half(q_raw, q_grouped, 1, 0, ev[Q1_EV])
+        transpose_half(q_raw, q_grouped, 1, 1, ev[Q1_EV])
         run_norms(FIRST_NORMS)
         for g in range(1, CHUNKS):
             regroup_v(g)
@@ -293,36 +373,56 @@ def tile_selfattention_pa_kernel(tc, q, k, v, out):
                 quantise_chunk(q_grouped, q_codes, q_scales, 1)
         quantise_chunk(v_grouped, v_codes, v_scales, CHUNKS - 1)
 
-        size = min(SPREAD_MAX, max(1, (FIRST_NORMS - CHAIN_UNITS) // CHUNKS))
-        spread_norms(range(size))
-        next_spread = size
+        spread_norms(columns[0:2])
+        next_spread = 2
+        row_tasks = []
+        for i, b in enumerate(ROW_BLOCKS):
+            at = ROW_START + 8 * i
+            row_tasks += [(at + g, lambda b=b, g=g: row_pass(b, g)) for g in range(CHUNKS)]
+            row_tasks.append((at + CHUNKS + 1, lambda b=b: (row_turn(b, 0), row_turn(b, 2))))
+            row_tasks.append((at + ROW_Q, lambda b=b: row_quantise(b)))
         outs_done = 0
-        stores_done = 0
-        store_after = {}
+        stored = 0
+        store_at = {}
 
         step = 0
-        while stores_done < BLOCKS:
-            if step < UNITS:
+        while stored < BLOCKS:
+            if step < w_units:
                 weight_pass(step)
-            if 1 <= step < UNITS + 1:
+            if 1 <= step < w_units + 1:
                 weight_quantise(step - 1)
             run_norms(FIRST_NORMS + (UNITS - FIRST_NORMS) * (step + 1) // NORM_SPAN)
             for g in (2, 3):
                 if step == Q_STEP + (g - 2) * Q_EVERY:
-                    turn_q(g)
+                    if (Q2_DVE, Q3_DVE)[g - 2]:
+                        turn_q(g)
+                    else:
+                        transpose_half(q_raw, q_grouped, g, 0, nc.scalar.copy)
+                        transpose_half(q_raw, q_grouped, g, 1, nc.vector.tensor_copy if Q_EV else nc.scalar.copy)
                 if step == Q_STEP + (g - 2) * Q_EVERY + 2:
                     quantise_chunk(q_grouped, q_codes, q_scales, g)
-            if next_spread < BLOCKS and step + SPREAD_AHEAD >= next_spread * CHUNKS:
-                ready = max((len(norms_done) - CHAIN_UNITS) // CHUNKS, next_spread + 1)
-                size = min(ready - next_spread, SPREAD_MAX)
-                spread_norms(range(next_spread, next_spread + size))
+            for at, task in row_tasks:
+                if at == step:
+                    task()
+            if next_spread < len(columns) and step + SPREAD_AHEAD >= next_spread * CHUNKS:
+                size = 1
+                while size < SPREAD_MAX and next_spread + size < len(columns) and norm_ready(columns[next_spread + size]):
+                    size += 1
+                spread_norms(columns[next_spread : next_spread + size])
                 next_spread += size
-            if outs_done < UNITS and outs_done <= step - OUT_LAG:
-                output_pass(outs_done)
-                if outs_done % CHUNKS == CHUNKS - 1:
-                    store_after[outs_done // CHUNKS] = step + STORE_LAG
-                outs_done += 1
-            if stores_done in store_after and step >= store_after[stores_done]:
-                store(stores_done)
-                stores_done += 1
+            for i in range(OUT_RATE):
+                if outs_done < UNITS:
+                    b, g = out_order[outs_done]
+                    if b in ROW_BLOCKS:
+                        ready = step > ROW_START + 8 * ROW_BLOCKS.index(b) + ROW_Q
+                    else:
+                        ready = columns.index(b) * CHUNKS + g <= step - OUT_LAG
+                    if ready:
+                        output_pass(b, g)
+                        if g == CHUNKS - 1:
+                            store_at[b] = step + STORE_LAG
+                        outs_done += 1
+            if stored < BLOCKS and out_blocks[stored] in store_at and step >= store_at[out_blocks[stored]]:
+                store(out_blocks[stored])
+                stored += 1
             step += 1

@@ -12,6 +12,7 @@ ALU = mybir.AluOpType
 ACT = mybir.ActivationFunctionType
 
 P = 128
+QUAD = 32
 PACK = 4
 CHUNK = P * PACK
 ROWS = 2048
@@ -22,39 +23,45 @@ UNITS = BLOCKS * CHUNKS
 EPS = 1e-12
 FLOPS = 2 * ROWS * ROWS * WIDTH * 2
 
-FIRST_NORMS = 13
-SPREAD_MAX = 2
-CHAIN_UNITS = 2
+FIRST_NORMS = 12
+SPREAD_MAX = 3
+CHAIN_UNITS = 4
 SPREAD_AHEAD = 1
-OUT_LAG = 4
-STORE_LAG = 1
-NORM_SPAN = 48
-Q1_AT = 9
-S_BOTH = (0, 1)
+OUT_LAG = 5
+STORE_LAG = 0
+NORM_SPAN = 46
+Q1_AT = 8
+S_BOTH = (0, 1, 2)
 Q1Q_AT = 3
 NB = 3
 WB = 3
 Q_STEP = 13
 Q_EVERY = 10
 ROW_BLOCKS = (15,)
-Q_UNITS = 1
+P_LO = 3
+P_HI = 0
+PARK_LAG = 2
+Q3_STEPS = (8, 12, 16, 20)
+END_SPLIT = 2
+ORDER = 'nwoqrsz'
+Q_UNITS = 2
 LAST_UNITS = 1
 Q2_DVE = 1
 Q3_DVE = 1
 S_REG = ()
-V_BOTH = ()
-Q_EV = 1
+V_BOTH = (2,)
+Q_EV = 0
 Q1_EV = 0
 Q23_AT = 2
-KW = 0
+KW = 1
 N_FIRST = 1
 REG0 = 0
-ROW_START = 50
+ROW_START = 49
 ROW_Q = 6
 O_BEFORE = 1
 N_BEFORE = 1
-Q01_EV = 1
-OUT_RATE = 1
+Q01_EV = 0
+OUT_RATE = 2
 WARM_UP = 5
 
 
@@ -163,6 +170,7 @@ def tile_selfattention_pa_kernel(tc, q, k, v, out):
 
         squares = {}
         inv_norm = {}
+        squared = {}
         spread = {}
         w_grouped = {}
         w_codes = {}
@@ -195,6 +203,18 @@ def tile_selfattention_pa_kernel(tc, q, k, v, out):
             )
             inv_norm[b] = small.tile([P, 1], F32, name="inv_norm")
             nc.gpsimd.tensor_tensor(out=inv_norm[b][:], in0=floored[:], in1=minus_half[:], op=ALU.pow)
+            if P_LO <= b < P_HI:
+                squared[b] = small.tile([P, QUAD], F32, name="squared", align_bytes=64)
+                nc.gpsimd.tensor_copy(out=squared[b][:], in_=inv_norm[b][:].to_broadcast([P, QUAD]))
+
+        def park_norm(b):
+            turned = small.tile([P, QUAD], F32, name="turned_norm", align_bytes=64)
+            nc.vector.transpose(turned[:], squared[b][:])
+            spot = out[b * P, 0:P]
+            nc.sync.dma_start(out=spot.rearrange("(s i) -> s i", i=QUAD), in_=turned[0:P:QUAD, :])
+            tile = small.tile([P, P], F32, name="spread_by_load")
+            nc.sync.dma_start(out=tile[:], in_=spot.partition_broadcast(P))
+            spread[b] = tile[:]
 
         def spread_norms(blocks):
             bank = ps_weight.tile([P, SPREAD_MAX, P], F32, tag="bank", name="spread_bank")
@@ -284,24 +304,31 @@ def tile_selfattention_pa_kernel(tc, q, k, v, out):
                 )
 
         def output_pass(b, g):
-            if g == 0:
-                acc[b] = ps_out.tile([P, WIDTH], F32, tag="acc", name="acc")
+            parts = 2 if END_SPLIT == 1 and b == out_blocks[-1] else 1
+            width = WIDTH // parts
             cols = slice(g * P, (g + 1) * P)
-            key_cols = slice(g * CHUNK, (g + 1) * CHUNK)
-            nc.tensor.matmul_mx(
-                out=acc[b][:],
-                lhsT=w_codes[b][:, cols].bitcast(FP8X4),
-                lhsT_scale=w_scales[b][:, cols],
-                rhs=v_codes[:, key_cols].bitcast(FP8X4),
-                rhs_scale=v_scales[:, key_cols],
-                start=(g == 0),
-                stop=(g == CHUNKS - 1),
-            )
+            for i in range(parts):
+                if g == 0:
+                    acc[b, i] = ps_out.tile([P, width], F32, tag="acc", name="acc")
+                key_cols = slice(g * CHUNK + i * width, g * CHUNK + (i + 1) * width)
+                nc.tensor.matmul_mx(
+                    out=acc[b, i][:],
+                    lhsT=w_codes[b][:, cols].bitcast(FP8X4),
+                    lhsT_scale=w_scales[b][:, cols],
+                    rhs=v_codes[:, key_cols].bitcast(FP8X4),
+                    rhs_scale=v_scales[:, key_cols],
+                    start=(g == 0),
+                    stop=(g == CHUNKS - 1),
+                )
 
         def store(b):
-            result = stage.tile([P, WIDTH], F32, name="result")
-            nc.scalar.copy(out=result[:], in_=acc[b][:])
-            nc.sync.dma_start(out=out_rows[:, b, :], in_=result[:])
+            parts = 2 if END_SPLIT and b == out_blocks[-1] else 1
+            width = WIDTH // parts
+            for i in range(parts):
+                result = stage.tile([P, width], F32, name="result")
+                src = acc[b, i][:] if END_SPLIT == 1 or parts == 1 else acc[b, 0][:, i * width : (i + 1) * width]
+                (nc.scalar.copy, nc.vector.tensor_copy if END_SPLIT == 1 else nc.scalar.copy)[i](out=result[:], in_=src)
+                nc.sync.dma_start(out=out_rows[:, b, i * width : (i + 1) * width], in_=result[:])
 
         columns = [b for b in range(BLOCKS) if b not in ROW_BLOCKS]
         cut_n, cut_o = len(columns) - N_BEFORE, len(columns) - O_BEFORE
@@ -334,15 +361,18 @@ def tile_selfattention_pa_kernel(tc, q, k, v, out):
         for g in range(CHUNKS):
             load(v_raw, v_rows, g)
         load_q(4, 8)
+        def load_turned_q(g, s):
+            nc.sync.dma_start(
+                out=q_raw[32 * s : 32 * s + 32, g * CHUNK * PACK : (g + 1) * CHUNK * PACK].rearrange("p (m i) -> p m i", i=64),
+                in_=q_seg[s, :, 32 * g : 32 * g + 32, :],
+            )
+
         for g in (2, 3):
             if not (Q2_DVE, Q3_DVE)[g - 2]:
                 load_q(4 * g, 4 * g + 4)
-                continue
-            for s in range(4):
-                nc.sync.dma_start(
-                    out=q_raw[32 * s : 32 * s + 32, g * CHUNK * PACK : (g + 1) * CHUNK * PACK].rearrange("p (m i) -> p m i", i=64),
-                    in_=q_seg[s, :, 32 * g : 32 * g + 32, :],
-                )
+            elif g == 2 or not Q3_STEPS:
+                for s in range(4):
+                    load_turned_q(g, s)
 
         ev = (nc.scalar.copy, nc.vector.tensor_copy)
         transpose_half(q_raw, q_grouped, 0, 0, ev[Q01_EV])
@@ -374,55 +404,68 @@ def tile_selfattention_pa_kernel(tc, q, k, v, out):
         quantise_chunk(v_grouped, v_codes, v_scales, CHUNKS - 1)
 
         spread_norms(columns[0:2])
-        next_spread = 2
         row_tasks = []
         for i, b in enumerate(ROW_BLOCKS):
             at = ROW_START + 8 * i
             row_tasks += [(at + g, lambda b=b, g=g: row_pass(b, g)) for g in range(CHUNKS)]
             row_tasks.append((at + CHUNKS + 1, lambda b=b: (row_turn(b, 0), row_turn(b, 2))))
             row_tasks.append((at + ROW_Q, lambda b=b: row_quantise(b)))
+        parks = [b for b in columns if P_LO <= b < P_HI]
+        turns = [b for b in columns[2:] if not P_LO <= b < P_HI]
         outs_done = 0
         stored = 0
         store_at = {}
 
         step = 0
         while stored < BLOCKS:
-            if step < w_units:
-                weight_pass(step)
-            if 1 <= step < w_units + 1:
-                weight_quantise(step - 1)
-            run_norms(FIRST_NORMS + (UNITS - FIRST_NORMS) * (step + 1) // NORM_SPAN)
-            for g in (2, 3):
-                if step == Q_STEP + (g - 2) * Q_EVERY:
-                    if (Q2_DVE, Q3_DVE)[g - 2]:
-                        turn_q(g)
-                    else:
-                        transpose_half(q_raw, q_grouped, g, 0, nc.scalar.copy)
-                        transpose_half(q_raw, q_grouped, g, 1, nc.vector.tensor_copy if Q_EV else nc.scalar.copy)
-                if step == Q_STEP + (g - 2) * Q_EVERY + 2:
-                    quantise_chunk(q_grouped, q_codes, q_scales, g)
-            for at, task in row_tasks:
-                if at == step:
-                    task()
-            if next_spread < len(columns) and step + SPREAD_AHEAD >= next_spread * CHUNKS:
-                size = 1
-                while size < SPREAD_MAX and next_spread + size < len(columns) and norm_ready(columns[next_spread + size]):
-                    size += 1
-                spread_norms(columns[next_spread : next_spread + size])
-                next_spread += size
-            for i in range(OUT_RATE):
-                if outs_done < UNITS:
-                    b, g = out_order[outs_done]
-                    if b in ROW_BLOCKS:
-                        ready = step > ROW_START + 8 * ROW_BLOCKS.index(b) + ROW_Q
-                    else:
-                        ready = columns.index(b) * CHUNKS + g <= step - OUT_LAG
-                    if ready:
-                        output_pass(b, g)
-                        if g == CHUNKS - 1:
-                            store_at[b] = step + STORE_LAG
-                        outs_done += 1
-            if stored < BLOCKS and out_blocks[stored] in store_at and step >= store_at[out_blocks[stored]]:
-                store(out_blocks[stored])
-                stored += 1
+            for part in ORDER:
+                if part == "w":
+                    if step < w_units:
+                        weight_pass(step)
+                    if 1 <= step < w_units + 1:
+                        weight_quantise(step - 1)
+                elif part == "n":
+                    run_norms(FIRST_NORMS + (UNITS - FIRST_NORMS) * (step + 1) // NORM_SPAN)
+                elif part == "q":
+                    if step in Q3_STEPS and Q3_DVE:
+                        load_turned_q(3, Q3_STEPS.index(step))
+                    while parks and len(norms_done) >= CHUNKS * (norm_blocks.index(parks[0]) + 1) + PARK_LAG:
+                        park_norm(parks.pop(0))
+                    for g in (2, 3):
+                        if step == Q_STEP + (g - 2) * Q_EVERY:
+                            if (Q2_DVE, Q3_DVE)[g - 2]:
+                                turn_q(g)
+                            else:
+                                transpose_half(q_raw, q_grouped, g, 0, nc.scalar.copy)
+                                transpose_half(q_raw, q_grouped, g, 1, nc.vector.tensor_copy if Q_EV else nc.scalar.copy)
+                        if step == Q_STEP + (g - 2) * Q_EVERY + 2:
+                            quantise_chunk(q_grouped, q_codes, q_scales, g)
+                elif part == "r":
+                    for at, task in row_tasks:
+                        if at == step:
+                            task()
+                elif part == "s":
+                    if turns and step + SPREAD_AHEAD >= columns.index(turns[0]) * CHUNKS:
+                        size = 1
+                        while size < SPREAD_MAX and size < len(turns) and norm_ready(turns[size]):
+                            size += 1
+                        spread_norms(turns[:size])
+                        turns = turns[size:]
+                elif part == "o":
+                    for i in range(OUT_RATE):
+                        if outs_done < UNITS:
+                            b, g = out_order[outs_done]
+                            if b in ROW_BLOCKS:
+                                ready = step > ROW_START + 8 * ROW_BLOCKS.index(b) + ROW_Q
+                            else:
+                                ready = columns.index(b) * CHUNKS + g <= step - OUT_LAG
+                            if ready:
+                                output_pass(b, g)
+                                if g == CHUNKS - 1:
+                                    store_at[b] = step + STORE_LAG
+                                outs_done += 1
+                elif part == "z":
+                    if stored < BLOCKS and out_blocks[stored] in store_at and step >= store_at[out_blocks[stored]]:
+                        store(out_blocks[stored])
+                        stored += 1
             step += 1

@@ -25,12 +25,12 @@ FLOPS = 2 * ROWS * ROWS * WIDTH * 2
 
 FIRST_NORMS = 12
 SPREAD_MAX = 3
-CHAIN_UNITS = 4
+CHAIN_UNITS = 5
 SPREAD_AHEAD = 1
 OUT_LAG = 5
-STORE_LAG = 0
+STORE_LAG = 1
 NORM_SPAN = 46
-Q1_AT = 8
+Q1_AT = 7
 S_BOTH = (0, 1, 2)
 Q1Q_AT = 3
 NB = 3
@@ -38,12 +38,15 @@ WB = 3
 Q_STEP = 13
 Q_EVERY = 10
 ROW_BLOCKS = (15,)
-P_LO = 3
+Z_MOD = 3
+SP_V = 0
+ROW_EV = 0
+P_LO = 6
 P_HI = 0
 PARK_LAG = 2
-Q3_STEPS = (8, 12, 16, 20)
+Q3_STEPS = (4, 8, 12, 16)
 END_SPLIT = 2
-ORDER = 'nwoqrsz'
+ORDER = 'nwsqroz'
 Q_UNITS = 2
 LAST_UNITS = 1
 Q2_DVE = 1
@@ -60,7 +63,7 @@ ROW_START = 49
 ROW_Q = 6
 O_BEFORE = 1
 N_BEFORE = 1
-Q01_EV = 0
+Q01_EV = 1
 OUT_RATE = 2
 WARM_UP = 5
 
@@ -222,7 +225,7 @@ def tile_selfattention_pa_kernel(tc, q, k, v, out):
             for i, b in enumerate(blocks):
                 nc.tensor.transpose(bank[:, i, :], inv_norm[b][:, 0:1].to_broadcast([P, P]), ident[:])
                 spread[b] = tile[:, i, :]
-            nc.scalar.copy(out=tile[:, 0 : len(blocks), :], in_=bank[:, 0 : len(blocks), :])
+            (nc.vector.tensor_copy if SP_V else nc.scalar.copy)(out=tile[:, 0 : len(blocks), :], in_=bank[:, 0 : len(blocks), :])
 
         w_rows = {}
 
@@ -255,7 +258,7 @@ def tile_selfattention_pa_kernel(tc, q, k, v, out):
                     first = ((g + i) * 2 + u) * P
                     nc.tensor.transpose(bank[:, i, u, :], words[:, first : first + P], ident[:])
             grouped_words = w_grouped[b][:].rearrange("p g r t -> p (g r t)").bitcast(F32)
-            nc.scalar.copy(
+            (nc.vector.tensor_copy if ROW_EV else nc.scalar.copy)(
                 out=grouped_words[:, g * 2 * P : (g + 2) * 2 * P].rearrange("p (g r u) -> p g r u", g=2, u=2),
                 in_=bank[:].rearrange("p g u r -> p g r u"),
             )
@@ -327,7 +330,7 @@ def tile_selfattention_pa_kernel(tc, q, k, v, out):
             for i in range(parts):
                 result = stage.tile([P, width], F32, name="result")
                 src = acc[b, i][:] if END_SPLIT == 1 or parts == 1 else acc[b, 0][:, i * width : (i + 1) * width]
-                (nc.scalar.copy, nc.vector.tensor_copy if END_SPLIT == 1 else nc.scalar.copy)[i](out=result[:], in_=src)
+                (nc.vector.tensor_copy if (Z_MOD and b % Z_MOD == Z_MOD - 1) or (i == 1 and END_SPLIT == 3) else nc.scalar.copy)(out=result[:], in_=src)
                 nc.sync.dma_start(out=out_rows[:, b, i * width : (i + 1) * width], in_=result[:])
 
         columns = [b for b in range(BLOCKS) if b not in ROW_BLOCKS]

from contextlib import ExitStack

import concourse.mybir as mybir
from concourse.masks import make_identity

F32 = mybir.dt.float32
BF16 = mybir.dt.bfloat16
U32 = mybir.dt.uint32
U8 = mybir.dt.uint8
FP8X4 = mybir.dt.float8_e4m3fn_x4
ALU = mybir.AluOpType
ACT = mybir.ActivationFunctionType

P = 128
QUAD = 32
PACK = 4
CHUNK = P * PACK
ROWS = 2048
WIDTH = 512
CHUNKS = ROWS // CHUNK
BLOCKS = ROWS // P
UNITS = BLOCKS * CHUNKS
EPS = 1e-12
FLOPS = 2 * ROWS * ROWS * WIDTH * 2

FIRST_NORMS = 12
SPREAD_MAX = 3
CHAIN_UNITS = 5
SPREAD_AHEAD = 1
OUT_LAG = 5
STORE_LAG = 1
NORM_SPAN = 46
Q1_AT = 7
S_BOTH = (0, 1, 2)
Q1Q_AT = 3
NB = 3
WB = 3
Q_STEP = 13
Q_EVERY = 10
ROW_BLOCKS = (15,)
Z_MOD = 3
SP_V = 0
ROW_EV = 0
P_LO = 6
P_HI = 0
PARK_LAG = 2
Q3_STEPS = (4, 8, 12, 16)
END_SPLIT = 2
ORDER = 'nwsqroz'
Q_UNITS = 2
LAST_UNITS = 1
Q2_DVE = 1
Q3_DVE = 1
S_REG = ()
V_BOTH = (2,)
Q_EV = 0
Q1_EV = 0
Q23_AT = 2
KW = 1
N_FIRST = 1
REG0 = 0
ROW_START = 49
ROW_Q = 6
O_BEFORE = 1
N_BEFORE = 1
Q01_EV = 1
OUT_RATE = 2
WARM_UP = 5


def tile_selfattention_pa_kernel(tc, q, k, v, out):
    nc = tc.nc
    with ExitStack() as ctx:
        keep = ctx.enter_context(tc.tile_pool(name="keep", bufs=1))
        small = ctx.enter_context(tc.tile_pool(name="small", bufs=24))
        scrap = ctx.enter_context(tc.tile_pool(name="scrap", bufs=4))
        weights = ctx.enter_context(tc.tile_pool(name="weights", bufs=4))
        stage = ctx.enter_context(tc.tile_pool(name="stage", bufs=8))
        ps_norm = ctx.enter_context(tc.psum_pool(name="ps_norm", bufs=NB))
        ps_weight = ctx.enter_context(tc.psum_pool(name="ps_weight", bufs=WB))
        ps_out = ctx.enter_context(tc.psum_pool(name="ps_out", bufs=2))

        ctx.enter_context(tc.manual_schedule())

        ident = keep.tile([P, P], F32, name="ident")
        make_identity(nc, ident[:])
        minus_half = keep.tile([P, 1], F32, name="minus_half")
        nc.gpsimd.memset(minus_half[:], -0.5)

        k_rows = k.rearrange("(g p t) d -> p g (t d)", p=P, t=PACK)
        v_rows = v.rearrange("(g p t) d -> p g (t d)", p=P, t=PACK)
        q_rows = q.rearrange("(b p) d -> p b d", p=P)
        out_rows = out.rearrange("(b p) d -> p b d", p=P)
        q_seg = q.rearrange("r (u s i) -> (r u) s i", u=2, s=4).rearrange("(m j) s i -> s j m i", j=32)

        q_raw = keep.tile([P, ROWS * PACK], BF16, name="q_raw", align_bytes=64)
        k_raw = keep.tile([P, ROWS * PACK], BF16, name="k_raw")
        v_raw = keep.tile([P, ROWS * PACK], BF16, name="v_raw")
        q_grouped = keep.tile([P, ROWS * PACK], BF16, name="q_grouped", align_bytes=64)
        k_grouped = keep.tile([P, ROWS * PACK], BF16, name="k_grouped", align_bytes=64)
        v_grouped = keep.tile([P, ROWS * PACK], BF16, name="v_grouped", align_bytes=64)
        q_codes = keep.tile([P, ROWS], U32, name="q_codes", align_bytes=64)
        k_codes = keep.tile([P, ROWS], U32, name="k_codes", align_bytes=64)
        v_codes = keep.tile([P, ROWS], U32, name="v_codes", align_bytes=64)
        q_scales = keep.tile([P, ROWS], U8, name="q_scales", align_bytes=64)
        k_scales = keep.tile([P, ROWS], U8, name="k_scales", align_bytes=64)
        v_scales = keep.tile([P, ROWS], U8, name="v_scales", align_bytes=64)

        idle = keep.tile([P, WIDTH], BF16, name="idle")
        nc.vector.memset(idle[:], 0.0)

        def keep_warm(count):
            for i in range(count):
                bank = ps_norm.tile([P, WIDTH], F32, tag="scores", name="unused")
                nc.tensor.matmul(bank[:], lhsT=idle[:, 0:P], rhs=idle[:], start=True, stop=True)

        keep_warm(WARM_UP)

        def load(raw, rows, g):
            nc.sync.dma_start(out=raw[:, g * CHUNK * PACK : (g + 1) * CHUNK * PACK], in_=rows[:, g, :])

        flips = [0]

        def flip_bank():
            flips[0] += 1
            if flips[0] <= 9 and flips[0] % 5 >= 3:
                return ps_out.tile([P, 2, 2 * P], F32, tag="acc", name="flipped_early")
            return ps_weight.tile([P, 2, 2 * P], F32, tag="bank", name="flipped")

        def transpose_half(raw, grouped, g, half, copy):
            raw_words = raw[:].bitcast(F32)
            grouped_words = grouped[:].bitcast(F32).rearrange("p (r u) -> p r u", u=2)
            bank = flip_bank()
            for t2 in range(2):
                first_word = (g * PACK + 2 * half + t2) * (WIDTH // 2)
                for u in range(2):
                    nc.tensor.transpose(
                        bank[:, u, t2 * P : (t2 + 1) * P],
                        raw_words[:, first_word + u * P : first_word + (u + 1) * P],
                        ident[:],
                    )
            first_col = g * CHUNK + half * 2 * P
            copy(
                out=grouped_words[:, first_col : first_col + 2 * P, :],
                in_=bank[:].rearrange("p u r -> p r u"),
            )

        def transpose_chunk(raw, grouped, g):
            transpose_half(raw, grouped, g, 0, nc.scalar.copy)
            transpose_half(raw, grouped, g, 1, nc.vector.tensor_copy)

        def quantise_cols(grouped, codes, scales, lo, hi):
            nc.vector.quantize_mx(
                out=codes[:, lo:hi].bitcast(FP8X4), scales=scales[:, lo:hi], in_=grouped[:, lo * PACK : hi * PACK]
            )

        def quantise_chunk(grouped, codes, scales, g):
            quantise_cols(grouped, codes, scales, g * CHUNK, (g + 1) * CHUNK)

        def regroup_v(g):
            part = slice(g * CHUNK * PACK, (g + 1) * CHUNK * PACK)
            (nc.scalar.copy if g in S_REG else nc.vector.tensor_copy)(
                out=v_grouped[:, part].rearrange("p (c i t) -> p c t i", i=4, t=PACK),
                in_=v_raw[:, part].rearrange("p (t c i) -> p c t i", i=4, t=PACK),
            )

        def turn_q(g):
            cols = slice(g * CHUNK * PACK, (g + 1) * CHUNK * PACK)
            nc.vector.transpose(q_grouped[:, cols].bitcast(F32), q_raw[:, cols].bitcast(F32))

        def query_cols(b):
            return slice(b * P, (b + 1) * P)

        squares = {}
        inv_norm = {}
        squared = {}
        spread = {}
        w_grouped = {}
        w_codes = {}
        w_scales = {}
        acc = {}

        def norm_pass(b, g):
            if b not in squares:
                squares[b] = small.tile([P, CHUNKS], F32, name="squares")
            key_cols = slice(g * CHUNK, (g + 1) * CHUNK)
            bank = ps_norm.tile([P, CHUNK], F32, tag="scores", name="scores")
            nc.tensor.matmul_mx(
                out=bank[:],
                lhsT=q_codes[:, query_cols(b)].bitcast(FP8X4),
                lhsT_scale=q_scales[:, query_cols(b)],
                rhs=k_codes[:, key_cols].bitcast(FP8X4),
                rhs_scale=k_scales[:, key_cols],
                start=True,
                stop=True,
            )
            unread = scrap.tile([P, CHUNK], BF16, name="unread")
            nc.scalar.activation(out=unread[:], in_=bank[:], func=ACT.Square, accum_out=squares[b][:, g : g + 1])

        def norm_finish(b):
            pair = small.tile([P, 2], F32, name="pair")
            nc.gpsimd.tensor_tensor(out=pair[:], in0=squares[b][:, 0:2], in1=squares[b][:, 2:4], op=ALU.add)
            floored = small.tile([P, 1], F32, name="floored")
            nc.gpsimd.tensor_scalar(
                out=floored[:], in0=pair[:, 0:1], scalar1=pair[:, 1:2], scalar2=EPS * EPS, op0=ALU.add, op1=ALU.max
            )
            inv_norm[b] = small.tile([P, 1], F32, name="inv_norm")
            nc.gpsimd.tensor_tensor(out=inv_norm[b][:], in0=floored[:], in1=minus_half[:], op=ALU.pow)
            if P_LO <= b < P_HI:
                squared[b] = small.tile([P, QUAD], F32, name="squared", align_bytes=64)
                nc.gpsimd.tensor_copy(out=squared[b][:], in_=inv_norm[b][:].to_broadcast([P, QUAD]))

        def park_norm(b):
            turned = small.tile([P, QUAD], F32, name="turned_norm", align_bytes=64)
            nc.vector.transpose(turned[:], squared[b][:])
            spot = out[b * P, 0:P]
            nc.sync.dma_start(out=spot.rearrange("(s i) -> s i", i=QUAD), in_=turned[0:P:QUAD, :])
            tile = small.tile([P, P], F32, name="spread_by_load")
            nc.sync.dma_start(out=tile[:], in_=spot.partition_broadcast(P))
            spread[b] = tile[:]

        def spread_norms(blocks):
            bank = ps_weight.tile([P, SPREAD_MAX, P], F32, tag="bank", name="spread_bank")
            tile = small.tile([P, SPREAD_MAX, P], F32, name="spread")
            for i, b in enumerate(blocks):
                nc.tensor.transpose(bank[:, i, :], inv_norm[b][:, 0:1].to_broadcast([P, P]), ident[:])
                spread[b] = tile[:, i, :]
            (nc.vector.tensor_copy if SP_V else nc.scalar.copy)(out=tile[:, 0 : len(blocks), :], in_=bank[:, 0 : len(blocks), :])

        w_rows = {}

        def row_pass(b, g):
            if g == 0:
                w_rows[b] = weights.tile([P, CHUNKS, 2, P, 2], BF16, name="w_rows", align_bytes=64)
                w_grouped[b] = weights.tile([P, CHUNKS, P, PACK], BF16, name="w_grouped", align_bytes=64)
                w_codes[b] = weights.tile([P, CHUNK], U32, name="w_codes", align_bytes=64)
                w_scales[b] = weights.tile([P, CHUNK], U8, name="w_scales", align_bytes=64)
            key_cols = slice(g * CHUNK, (g + 1) * CHUNK)
            bank = ps_norm.tile([P, CHUNK], F32, tag="scores", name="scores")
            nc.tensor.matmul_mx(
                out=bank[:],
                lhsT=q_codes[:, query_cols(b)].bitcast(FP8X4),
                lhsT_scale=q_scales[:, query_cols(b)],
                rhs=k_codes[:, key_cols].bitcast(FP8X4),
                rhs_scale=k_scales[:, key_cols],
                start=True,
                stop=True,
            )
            for u in range(2):
                half = bank[:, u * 2 * P : (u + 1) * 2 * P].rearrange("q (e p) -> q p e", e=2)
                nc.scalar.activation(out=w_rows[b][:, g, u, :, :], in_=half, func=ACT.Copy, scale=inv_norm[b][:])

        def row_turn(b, g):
            words = w_rows[b][:].rearrange("q g u p e -> q (g u p e)").bitcast(F32)
            bank = ps_norm.tile([P, 2, 2, P], F32, tag="scores", name="turned")
            for i in range(2):
                for u in range(2):
                    first = ((g + i) * 2 + u) * P
                    nc.tensor.transpose(bank[:, i, u, :], words[:, first : first + P], ident[:])
            grouped_words = w_grouped[b][:].rearrange("p g r t -> p (g r t)").bitcast(F32)
            (nc.vector.tensor_copy if ROW_EV else nc.scalar.copy)(
                out=grouped_words[:, g * 2 * P : (g + 2) * 2 * P].rearrange("p (g r u) -> p g r u", g=2, u=2),
                in_=bank[:].rearrange("p g u r -> p g r u"),
            )

        def row_quantise(b):
            nc.vector.quantize_mx(
                out=w_codes[b][:].bitcast(FP8X4),
                scales=w_scales[b][:],
                in_=w_grouped[b][:].rearrange("p g r t -> p (g r t)"),
            )

        def weight_pass(unit):
            b, g = columns[unit // CHUNKS], unit % CHUNKS
            if g == 0:
                w_grouped[b] = weights.tile([P, CHUNKS, P, PACK], BF16, name="w_grouped", align_bytes=64)
                w_codes[b] = weights.tile([P, CHUNK], U32, name="w_codes", align_bytes=64)
                w_scales[b] = weights.tile([P, CHUNK], U8, name="w_scales", align_bytes=64)
            bank = ps_weight.tile([P, PACK, P], F32, tag="bank", name="scores_t")
            for t in range(PACK):
                key_cols = slice(g * CHUNK + t * P, g * CHUNK + (t + 1) * P)
                nc.tensor.matmul_mx(
                    out=bank[:, t, :],
                    lhsT=k_codes[:, key_cols].bitcast(FP8X4),
                    lhsT_scale=k_scales[:, key_cols],
                    rhs=q_codes[:, query_cols(b)].bitcast(FP8X4),
                    rhs_scale=q_scales[:, query_cols(b)],
                    start=True,
                    stop=True,
                )
            nc.vector.tensor_tensor(
                out=w_grouped[b][:, g, :, :],
                in0=bank[:].rearrange("p t r -> p r t"),
                in1=spread[b].unsqueeze(2).to_broadcast([P, P, PACK]),
                op=ALU.mult,
            )

        def weight_quantise(unit):
            b, g = columns[unit // CHUNKS], unit % CHUNKS
            size = LAST_UNITS if b == columns[-1] else Q_UNITS
            if (g + 1) % size == 0:
                lo, hi = g + 1 - size, g + 1
                nc.vector.quantize_mx(
                    out=w_codes[b][:, lo * P : hi * P].bitcast(FP8X4),
                    scales=w_scales[b][:, lo * P : hi * P],
                    in_=w_grouped[b][:, lo:hi, :, :].rearrange("p g r t -> p (g r t)"),
                )

        def output_pass(b, g):
            parts = 2 if END_SPLIT == 1 and b == out_blocks[-1] else 1
            width = WIDTH // parts
            cols = slice(g * P, (g + 1) * P)
            for i in range(parts):
                if g == 0:
                    acc[b, i] = ps_out.tile([P, width], F32, tag="acc", name="acc")
                key_cols = slice(g * CHUNK + i * width, g * CHUNK + (i + 1) * width)
                nc.tensor.matmul_mx(
                    out=acc[b, i][:],
                    lhsT=w_codes[b][:, cols].bitcast(FP8X4),
                    lhsT_scale=w_scales[b][:, cols],
                    rhs=v_codes[:, key_cols].bitcast(FP8X4),
                    rhs_scale=v_scales[:, key_cols],
                    start=(g == 0),
                    stop=(g == CHUNKS - 1),
                )

        def store(b):
            parts = 2 if END_SPLIT and b == out_blocks[-1] else 1
            width = WIDTH // parts
            for i in range(parts):
                result = stage.tile([P, width], F32, name="result")
                src = acc[b, i][:] if END_SPLIT == 1 or parts == 1 else acc[b, 0][:, i * width : (i + 1) * width]
                (nc.vector.tensor_copy if (Z_MOD and b % Z_MOD == Z_MOD - 1) or (i == 1 and END_SPLIT == 3) else nc.scalar.copy)(out=result[:], in_=src)
                nc.sync.dma_start(out=out_rows[:, b, i * width : (i + 1) * width], in_=result[:])

        columns = [b for b in range(BLOCKS) if b not in ROW_BLOCKS]
        cut_n, cut_o = len(columns) - N_BEFORE, len(columns) - O_BEFORE
        norm_blocks = columns[:cut_n] + list(ROW_BLOCKS) + columns[cut_n:]
        out_blocks = columns[:cut_o] + list(ROW_BLOCKS) + columns[cut_o:]
        w_units = len(columns) * CHUNKS
        norm_order = [(b, g) for b in norm_blocks for g in range(CHUNKS)]
        out_order = [(b, g) for b in out_blocks for g in range(CHUNKS)]

        def norm_ready(b):
            return len(norms_done) >= CHUNKS * (norm_blocks.index(b) + 1) + CHAIN_UNITS

        norms_done = []

        def run_norms(count):
            while len(norms_done) < min(count, UNITS):
                b, g = norm_order[len(norms_done)]
                norm_pass(b, g)
                norms_done.append((b, g))
                if g == CHUNKS - 1:
                    norm_finish(b)

        def load_q(b0, b1):
            nc.sync.dma_start(out=q_raw[:, b0 * WIDTH : b1 * WIDTH].rearrange("p (b d) -> p b d", d=WIDTH), in_=q_rows[:, b0:b1, :])

        load_q(0, 2)
        for g in range(CHUNKS):
            load(k_raw, k_rows, g)
        load_q(2, 4)
        for g in range(CHUNKS):
            load(v_raw, v_rows, g)
        load_q(4, 8)
        def load_turned_q(g, s):
            nc.sync.dma_start(
                out=q_raw[32 * s : 32 * s + 32, g * CHUNK * PACK : (g + 1) * CHUNK * PACK].rearrange("p (m i) -> p m i", i=64),
                in_=q_seg[s, :, 32 * g : 32 * g + 32, :],
            )

        for g in (2, 3):
            if not (Q2_DVE, Q3_DVE)[g - 2]:
                load_q(4 * g, 4 * g + 4)
            elif g == 2 or not Q3_STEPS:
                for s in range(4):
                    load_turned_q(g, s)

        ev = (nc.scalar.copy, nc.vector.tensor_copy)
        transpose_half(q_raw, q_grouped, 0, 0, ev[Q01_EV])
        quantise_cols(q_grouped, q_codes, q_scales, 0, 2 * P)
        for g in range(CHUNKS):
            keep_warm(KW)
            transpose_half(k_raw, k_grouped, g, 0, ev[1] if g in V_BOTH else ev[0])
            transpose_half(k_raw, k_grouped, g, 1, ev[0] if g in S_BOTH else ev[1])
            if g >= 1:
                quantise_chunk(k_grouped, k_codes, k_scales, g - 1)
        run_norms(N_FIRST)
        quantise_chunk(k_grouped, k_codes, k_scales, CHUNKS - 1)
        if REG0 == 0:
            regroup_v(0)
        run_norms(Q23_AT)
        transpose_half(q_raw, q_grouped, 0, 1, ev[0])
        quantise_cols(q_grouped, q_codes, q_scales, 2 * P, 4 * P)
        if REG0 == 1:
            regroup_v(0)
        run_norms(Q1_AT + 1)
        transpose_half(q_raw, q_grouped, 1, 0, ev[Q1_EV])
        transpose_half(q_raw, q_grouped, 1, 1, ev[Q1_EV])
        run_norms(FIRST_NORMS)
        for g in range(1, CHUNKS):
            regroup_v(g)
            quantise_chunk(v_grouped, v_codes, v_scales, g - 1)
            if g == Q1Q_AT:
                quantise_chunk(q_grouped, q_codes, q_scales, 1)
        quantise_chunk(v_grouped, v_codes, v_scales, CHUNKS - 1)

        spread_norms(columns[0:2])
        row_tasks = []
        for i, b in enumerate(ROW_BLOCKS):
            at = ROW_START + 8 * i
            row_tasks += [(at + g, lambda b=b, g=g: row_pass(b, g)) for g in range(CHUNKS)]
            row_tasks.append((at + CHUNKS + 1, lambda b=b: (row_turn(b, 0), row_turn(b, 2))))
            row_tasks.append((at + ROW_Q, lambda b=b: row_quantise(b)))
        parks = [b for b in columns if P_LO <= b < P_HI]
        turns = [b for b in columns[2:] if not P_LO <= b < P_HI]
        outs_done = 0
        stored = 0
        store_at = {}

        step = 0
        while stored < BLOCKS:
            for part in ORDER:
                if part == "w":
                    if step < w_units:
                        weight_pass(step)
                    if 1 <= step < w_units + 1:
                        weight_quantise(step - 1)
                elif part == "n":
                    run_norms(FIRST_NORMS + (UNITS - FIRST_NORMS) * (step + 1) // NORM_SPAN)
                elif part == "q":
                    if step in Q3_STEPS and Q3_DVE:
                        load_turned_q(3, Q3_STEPS.index(step))
                    while parks and len(norms_done) >= CHUNKS * (norm_blocks.index(parks[0]) + 1) + PARK_LAG:
                        park_norm(parks.pop(0))
                    for g in (2, 3):
                        if step == Q_STEP + (g - 2) * Q_EVERY:
                            if (Q2_DVE, Q3_DVE)[g - 2]:
                                turn_q(g)
                            else:
                                transpose_half(q_raw, q_grouped, g, 0, nc.scalar.copy)
                                transpose_half(q_raw, q_grouped, g, 1, nc.vector.tensor_copy if Q_EV else nc.scalar.copy)
                        if step == Q_STEP + (g - 2) * Q_EVERY + 2:
                            quantise_chunk(q_grouped, q_codes, q_scales, g)
                elif part == "r":
                    for at, task in row_tasks:
                        if at == step:
                            task()
                elif part == "s":
                    if turns and step + SPREAD_AHEAD >= columns.index(turns[0]) * CHUNKS:
                        size = 1
                        while size < SPREAD_MAX and size < len(turns) and norm_ready(turns[size]):
                            size += 1
                        spread_norms(turns[:size])
                        turns = turns[size:]
                elif part == "o":
                    for i in range(OUT_RATE):
                        if outs_done < UNITS:
                            b, g = out_order[outs_done]
                            if b in ROW_BLOCKS:
                                ready = step > ROW_START + 8 * ROW_BLOCKS.index(b) + ROW_Q
                            else:
                                ready = columns.index(b) * CHUNKS + g <= step - OUT_LAG
                            if ready:
                                output_pass(b, g)
                                if g == CHUNKS - 1:
                                    store_at[b] = step + STORE_LAG
                                outs_done += 1
                elif part == "z":
                    if stored < BLOCKS and out_blocks[stored] in store_at and step >= store_at[out_blocks[stored]]:
                        store(out_blocks[stored])
                        stored += 1
            step += 1
